import numpy as np
import ml_dtypes

BF16 = ml_dtypes.bfloat16


def bf(x):
    return np.asarray(x, np.float32).astype(BF16)


def f32(x):
    return np.asarray(x, np.float32)


def f64(x):
    return np.asarray(x).astype(np.float64)


def striped(idx):
    return np.tile(idx.reshape(-1, 16).T, (8, 1))


C, S, T, K, N = 1024, 2048, 128, 8, 1024
BETA, ALPHA, MAX_DIST, EPS = 0.2, 0.3, 250.0, 1e-8


def setup_inputs():
    return {"x": f32(np.random.standard_normal((C, S))), "wna": bf(0.05 * np.random.standard_normal((C, C))), "offs": striped(np.random.permutation(np.tile(np.arange(S), 2))[:N])}


def reference(x, wna, offs):
    idx = offs[:16].T.reshape(-1)
    xs = f64(x)
    nbr = xs[:, idx]
    neg_target = -np.repeat(xs[:, :T], K, axis=1)
    diff = nbr + neg_target
    dist = np.sqrt(np.sum(diff * diff, axis=0))
    dw = np.exp(-ALPHA * dist / (MAX_DIST + EPS))
    z = ((f64(wna).T @ nbr) * dw[None, :]).reshape(C, T, K)
    e = np.exp(z - z.max(axis=2, keepdims=True))
    att = e / e.sum(axis=2, keepdims=True)
    return (1.0 - BETA) * np.sum(att * nbr.reshape(C, T, K), axis=2)

@@ -1,0 +1,144 @@
+import concourse.mybir as mybir
+
+F32 = mybir.dt.float32
+BF16 = mybir.dt.bfloat16
+U16 = mybir.dt.uint16
+ALU = mybir.AluOpType
+ACT = mybir.ActivationFunctionType
+AXIS = mybir.AxisListType
+
+P = 128
+C = 1024
+S = 2048
+T = 128
+K = 8
+N = T * K
+BLOCKS = C // P
+BANK = 512
+HALVES = N // BANK
+AHEAD = 3
+
+BETA, ALPHA, MAX_DIST, EPS = 0.2, 0.3, 250.0, 1e-8
+
+FLOPS = 2 * C * C * N
+
+
+def tile_graphattentionencoder_kernel(tc, x, wna, offs, out):
+    nc = tc.nc
+    with (
+        tc.tile_pool(name="held", bufs=1) as held,
+        tc.tile_pool(name="work", bufs=2) as work,
+        tc.tile_pool(name="small", bufs=2) as small,
+        tc.psum_pool(name="dist_banks", bufs=1) as dist_banks,
+        tc.psum_pool(name="score_banks", bufs=AHEAD) as score_banks,
+    ):
+        offsets = held.tile([P, N // 16], U16, name="offsets")
+        nc.sync.dma_start(offsets[:], offs)
+        x_blk = [held.tile([P, S], F32, name=f"x{c}") for c in range(BLOCKS)]
+        w_blk = [held.tile([P, C], BF16, name=f"w{c}") for c in range(BLOCKS)]
+        for c in range(BLOCKS):
+            nc.sync.dma_start(x_blk[c][:], x[c * P : (c + 1) * P, :])
+            nc.sync.dma_start(w_blk[c][:], wna[c * P : (c + 1) * P, :])
+
+        ones = held.tile([P, P], BF16, name="ones")
+        nc.gpsimd.memset(ones[:], 1.0)
+
+        def per_target(tile_pn):
+            return tile_pn.rearrange("p (t k) -> p t k", k=K)
+
+        def over_neighbours(tile_pt):
+            return tile_pt.unsqueeze(2).to_broadcast([P, T, K])
+
+        def new_score_banks(d):
+            return [
+                score_banks.tile([P, BANK], F32, name=f"y{d}_{h}", tag=f"y{h}")
+                for h in range(HALVES)
+            ]
+
+        def score_matmuls(y, d, c):
+            for h in range(HALVES):
+                nc.tensor.matmul(
+                    y[h][:],
+                    w_blk[c][:, d * P : (d + 1) * P],
+                    nbr[c][:, h * BANK : (h + 1) * BANK],
+                    start=(c == 0),
+                    stop=(c == BLOCKS - 1),
+                )
+
+        dist2 = [dist_banks.tile([P, BANK], F32, name=f"dist2_{h}") for h in range(HALVES)]
+        nbr = [held.tile([P, N], BF16, name=f"nbr{c}") for c in range(BLOCKS)]
+        raw = {d: new_score_banks(d) for d in range(AHEAD)}
+        for c in range(BLOCKS):
+            neg_target = work.tile([P, N], F32, name="neg_target")
+            nc.scalar.mul(per_target(neg_target[:]), over_neighbours(x_blk[c][:, 0:T]), -1.0)
+            diff = work.tile([P, N], F32, name="diff")
+            nc.vector.tensor_tensor(
+                diff[:], x_blk[c][:].indirect(offsets[:]), neg_target[:], ALU.add
+            )
+            square = work.tile([P, N], BF16, name="square")
+            nc.scalar.activation(square[:], diff[:], ACT.Square)
+            nc.vector.tensor_tensor(nbr[c][:], diff[:], neg_target[:], ALU.subtract)
+            for h in range(HALVES):
+                nc.tensor.matmul(
+                    dist2[h][:],
+                    ones[:],
+                    square[:, h * BANK : (h + 1) * BANK],
+                    start=(c == 0),
+                    stop=(c == BLOCKS - 1),
+                )
+            for d in range(AHEAD):
+                score_matmuls(raw[d], d, c)
+
+        dist = held.tile([P, N], F32, name="dist")
+        damp = held.tile([P, N], F32, name="damp")
+        for h in range(HALVES):
+            nc.scalar.activation(dist[:, h * BANK : (h + 1) * BANK], dist2[h][:], ACT.Sqrt)
+        for h in range(HALVES):
+            cols = slice(h * BANK, (h + 1) * BANK)
+            nc.scalar.activation(
+                damp[:, cols], dist[:, cols], ACT.Exp, scale=-ALPHA / (MAX_DIST + EPS)
+            )
+
+        def weights(d):
+            z = work.tile([P, N], F32, name="z")
+            for h in range(HALVES):
+                cols = slice(h * BANK, (h + 1) * BANK)
+                nc.vector.tensor_tensor(z[:, cols], raw[d][h][:], damp[:, cols], ALU.mult)
+            top = small.tile([P, T], F32, name="top")
+            nc.vector.tensor_reduce(top[:], per_target(z[:]), axis=AXIS.X, op=ALU.max)
+            shifted = work.tile([P, N], F32, name="shifted")
+            nc.vector.tensor_tensor(
+                per_target(shifted[:]), per_target(z[:]), over_neighbours(top[:]), ALU.subtract
+            )
+            e = work.tile([P, N], F32, name="e")
+            nc.scalar.activation(e[:], shifted[:], ACT.Exp)
+            return e
+
+        def attend(d, e):
+            total = small.tile([P, T], F32, name="total")
+            nc.vector.tensor_reduce(total[:], per_target(e[:]), axis=AXIS.X, op=ALU.add)
+            log_total = small.tile([P, T], F32, name="log_total")
+            nc.scalar.activation(log_total[:], total[:], ACT.Ln)
+            inverse = small.tile([P, T], F32, name="inverse")
+            nc.scalar.activation(inverse[:], log_total[:], ACT.Exp, scale=-1.0)
+            weighted = work.tile([P, N], F32, name="weighted")
+            nc.vector.tensor_tensor(
+                weighted[:], x_blk[d][:].indirect(offsets[:]), e[:], ALU.mult
+            )
+            summed = small.tile([P, T], F32, name="summed")
+            nc.vector.tensor_reduce(summed[:], per_target(weighted[:]), axis=AXIS.X, op=ALU.add)
+            result = small.tile([P, T], F32, name="result")
+            nc.vector.scalar_tensor_tensor(
+                result[:], summed[:], 1.0 - BETA, inverse[:], ALU.mult, ALU.mult
+            )
+            nc.sync.dma_start(out[d * P : (d + 1) * P, :], result[:])
+
+        e_of = {0: weights(0)}
+        for d in range(BLOCKS):
+            if d + AHEAD < BLOCKS:
+                raw[d + AHEAD] = new_score_banks(d + AHEAD)
+                for c in range(BLOCKS):
+                    score_matmuls(raw[d + AHEAD], d + AHEAD, c)
+            if d + 1 < BLOCKS:
+                e_of[d + 1] = weights(d + 1)
+            attend(d, e_of[d])

@@ -107,7 +107,7 @@ def tile_graphattentionencoder_kernel(tc, x, wna, offs, out):
             top = small.tile([P, T], F32, name="top")
             nc.vector.tensor_reduce(top[:], per_target(z[:]), axis=AXIS.X, op=ALU.max)
             shifted = work.tile([P, N], F32, name="shifted")
-            nc.vector.tensor_tensor(
+            nc.gpsimd.tensor_tensor(
                 per_target(shifted[:]), per_target(z[:]), over_neighbours(top[:]), ALU.subtract
             )
             e = work.tile([P, N], F32, name="e")

@@ -1,4 +1,5 @@
 import concourse.mybir as mybir
+from concourse.masks import make_identity
 
 F32 = mybir.dt.float32
 BF16 = mybir.dt.bfloat16
@@ -17,6 +18,8 @@ BLOCKS = C // P
 BANK = 512
 HALVES = N // BANK
 AHEAD = 3
+GROUP = BANK // P
+LATE = 5
 
 BETA, ALPHA, MAX_DIST, EPS = 0.2, 0.3, 250.0, 1e-8
 
@@ -27,9 +30,9 @@ def tile_graphattentionencoder_kernel(tc, x, wna, offs, out):
     nc = tc.nc
     with (
         tc.tile_pool(name="held", bufs=1) as held,
+        tc.tile_pool(name="diffs", bufs=LATE + 2) as diffs,
         tc.tile_pool(name="work", bufs=2) as work,
-        tc.tile_pool(name="small", bufs=2) as small,
-        tc.psum_pool(name="dist_banks", bufs=1) as dist_banks,
+        tc.psum_pool(name="side_banks", bufs=2) as side_banks,
         tc.psum_pool(name="score_banks", bufs=AHEAD) as score_banks,
     ):
         offsets = held.tile([P, N // 16], U16, name="offsets")
@@ -37,11 +40,15 @@ def tile_graphattentionencoder_kernel(tc, x, wna, offs, out):
         x_blk = [held.tile([P, S], F32, name=f"x{c}") for c in range(BLOCKS)]
         w_blk = [held.tile([P, C], BF16, name=f"w{c}") for c in range(BLOCKS)]
         for c in range(BLOCKS):
-            nc.sync.dma_start(x_blk[c][:], x[c * P : (c + 1) * P, :])
-            nc.sync.dma_start(w_blk[c][:], wna[c * P : (c + 1) * P, :])
+            queue = nc.sync if c % 2 == 0 else nc.scalar
+            queue.dma_start(x_blk[c][:], x[c * P : (c + 1) * P, :])
+        for c in range(BLOCKS):
+            nc.gpsimd.dma_start(w_blk[c][:], wna[c * P : (c + 1) * P, :])
 
         ones = held.tile([P, P], BF16, name="ones")
         nc.gpsimd.memset(ones[:], 1.0)
+        identity = held.tile([P, P], F32, name="identity")
+        make_identity(nc, identity[:])
 
         def per_target(tile_pn):
             return tile_pn.rearrange("p (t k) -> p t k", k=K)
@@ -49,96 +56,159 @@ def tile_graphattentionencoder_kernel(tc, x, wna, offs, out):
         def over_neighbours(tile_pt):
             return tile_pt.unsqueeze(2).to_broadcast([P, T, K])
 
+        def halves():
+            return [slice(h * BANK, (h + 1) * BANK) for h in range(HALVES)]
+
         def new_score_banks(d):
             return [
-                score_banks.tile([P, BANK], F32, name=f"y{d}_{h}", tag=f"y{h}")
+                score_banks.tile([P, BANK], F32, name=f"raw{d}_{h}", tag=f"raw{h}")
                 for h in range(HALVES)
             ]
 
-        def score_matmuls(y, d, c):
-            for h in range(HALVES):
+        def score_matmuls(d, c):
+            for h, cols in enumerate(halves()):
                 nc.tensor.matmul(
-                    y[h][:],
+                    raw[d][h][:],
                     w_blk[c][:, d * P : (d + 1) * P],
-                    nbr[c][:, h * BANK : (h + 1) * BANK],
+                    nbr[c][:, cols],
                     start=(c == 0),
                     stop=(c == BLOCKS - 1),
                 )
 
-        dist2 = [dist_banks.tile([P, BANK], F32, name=f"dist2_{h}") for h in range(HALVES)]
+        dist2 = [
+            side_banks.tile([P, BANK], F32, name=f"dist2_{h}", tag="side") for h in range(HALVES)
+        ]
         nbr = [held.tile([P, N], BF16, name=f"nbr{c}") for c in range(BLOCKS)]
         raw = {d: new_score_banks(d) for d in range(AHEAD)}
-        for c in range(BLOCKS):
-            neg_target = work.tile([P, N], F32, name="neg_target")
-            nc.scalar.mul(per_target(neg_target[:]), over_neighbours(x_blk[c][:, 0:T]), -1.0)
-            diff = work.tile([P, N], F32, name="diff")
+        neg_target = {}
+        diff = {}
+
+        def negate_target(c):
+            neg_target[c] = work.tile([P, N], F32, name=f"neg_target{c}", tag="neg_target", bufs=3)
+            nc.scalar.mul(per_target(neg_target[c][:]), over_neighbours(x_blk[c][:, 0:T]), -1.0)
+
+        def look_up_diff(c):
+            diff[c] = diffs.tile([P, N], F32, name=f"diff{c}", tag="diff")
             nc.vector.tensor_tensor(
-                diff[:], x_blk[c][:].indirect(offsets[:]), neg_target[:], ALU.add
+                diff[c][:], x_blk[c][:].indirect(offsets[:]), neg_target[c][:], ALU.add
             )
+
+        def sum_squares(c):
             square = work.tile([P, N], BF16, name="square")
-            nc.scalar.activation(square[:], diff[:], ACT.Square)
-            nc.vector.tensor_tensor(nbr[c][:], diff[:], neg_target[:], ALU.subtract)
-            for h in range(HALVES):
+            nc.scalar.activation(square[:], diff[c][:], ACT.Square)
+            for h, cols in enumerate(halves()):
                 nc.tensor.matmul(
-                    dist2[h][:],
-                    ones[:],
-                    square[:, h * BANK : (h + 1) * BANK],
-                    start=(c == 0),
-                    stop=(c == BLOCKS - 1),
+                    dist2[h][:], ones[:], square[:, cols], start=(c == 0), stop=(c == BLOCKS - 1)
                 )
-            for d in range(AHEAD):
-                score_matmuls(raw[d], d, c)
+
+        def pick(c):
+            nc.vector.tensor_tensor(
+                per_target(nbr[c][:]),
+                per_target(diff[c][:]),
+                over_neighbours(x_blk[c][:, 0:T]),
+                ALU.add,
+            )
+
+        negate_target(0)
+        negate_target(1)
+        for c in range(BLOCKS):
+            look_up_diff(c)
+            if c + 2 < BLOCKS:
+                negate_target(c + 2)
+            sum_squares(c)
+            if c >= LATE:
+                pick(c - LATE)
+                for d in range(AHEAD):
+                    score_matmuls(d, c - LATE)
+        for c in range(BLOCKS - LATE, BLOCKS):
+            pick(c)
+        for d in range(AHEAD):
+            for c in range(BLOCKS - LATE, BLOCKS):
+                score_matmuls(d, c)
 
         dist = held.tile([P, N], F32, name="dist")
         damp = held.tile([P, N], F32, name="damp")
-        for h in range(HALVES):
-            nc.scalar.activation(dist[:, h * BANK : (h + 1) * BANK], dist2[h][:], ACT.Sqrt)
-        for h in range(HALVES):
-            cols = slice(h * BANK, (h + 1) * BANK)
+        for h, cols in enumerate(halves()):
+            nc.scalar.activation(dist[:, cols], dist2[h][:], ACT.Sqrt)
+        for cols in halves():
             nc.scalar.activation(
                 damp[:, cols], dist[:, cols], ACT.Exp, scale=-ALPHA / (MAX_DIST + EPS)
             )
 
+        total = {}
+        summed = {}
+        inverse = {}
+
+        def sum_over_neighbours(bank, d, tile_pn):
+            for k in range(K):
+                nc.tensor.matmul(
+                    bank[:, (d % GROUP) * P : (d % GROUP + 1) * P],
+                    per_target(tile_pn[:])[:, :, k],
+                    identity[:],
+                    is_transpose=True,
+                    start=(k == 0),
+                    stop=(k == K - 1),
+                )
+
         def weights(d):
             z = work.tile([P, N], F32, name="z")
-            for h in range(HALVES):
-                cols = slice(h * BANK, (h + 1) * BANK)
+            for h, cols in enumerate(halves()):
                 nc.vector.tensor_tensor(z[:, cols], raw[d][h][:], damp[:, cols], ALU.mult)
-            top = small.tile([P, T], F32, name="top")
+            top = work.tile([P, T], F32, name="top")
             nc.vector.tensor_reduce(top[:], per_target(z[:]), axis=AXIS.X, op=ALU.max)
             shifted = work.tile([P, N], F32, name="shifted")
-            nc.gpsimd.tensor_tensor(
+            nc.vector.tensor_tensor(
                 per_target(shifted[:]), per_target(z[:]), over_neighbours(top[:]), ALU.subtract
             )
             e = work.tile([P, N], F32, name="e")
             nc.scalar.activation(e[:], shifted[:], ACT.Exp)
+            g = d // GROUP
+            if d % GROUP == 0:
+                total[g] = side_banks.tile([P, BANK], F32, name=f"total{g}", tag="side")
+            sum_over_neighbours(total[g], d, e)
+            if d % GROUP == GROUP - 1:
+                log_total = work.tile([P, BANK], F32, name="log_total")
+                nc.scalar.activation(log_total[:], total[g][:], ACT.Ln)
+                inverse[g] = work.tile([P, BANK], F32, name=f"inverse{g}", tag="inverse")
+                nc.scalar.activation(inverse[g][:], log_total[:], ACT.Exp, scale=-1.0)
             return e
 
         def attend(d, e):
-            total = small.tile([P, T], F32, name="total")
-            nc.vector.tensor_reduce(total[:], per_target(e[:]), axis=AXIS.X, op=ALU.add)
-            log_total = small.tile([P, T], F32, name="log_total")
-            nc.scalar.activation(log_total[:], total[:], ACT.Ln)
-            inverse = small.tile([P, T], F32, name="inverse")
-            nc.scalar.activation(inverse[:], log_total[:], ACT.Exp, scale=-1.0)
             weighted = work.tile([P, N], F32, name="weighted")
             nc.vector.tensor_tensor(
                 weighted[:], x_blk[d][:].indirect(offsets[:]), e[:], ALU.mult
             )
-            summed = small.tile([P, T], F32, name="summed")
-            nc.vector.tensor_reduce(summed[:], per_target(weighted[:]), axis=AXIS.X, op=ALU.add)
-            result = small.tile([P, T], F32, name="result")
+            g = d // GROUP
+            if d % GROUP == 0:
+                summed[g] = side_banks.tile([P, BANK], F32, name=f"summed{g}", tag="side")
+            sum_over_neighbours(summed[g], d, weighted)
+
+        def finish(g):
+            result = work.tile([P, BANK], F32, name="result")
             nc.vector.scalar_tensor_tensor(
-                result[:], summed[:], 1.0 - BETA, inverse[:], ALU.mult, ALU.mult
+                result[:], summed[g][:], 1.0 - BETA, inverse[g][:], ALU.mult, ALU.mult
             )
-            nc.sync.dma_start(out[d * P : (d + 1) * P, :], result[:])
+            turned = score_banks.tile([P, BANK], F32, name=f"turned{g}", tag="raw0")
+            for i in range(GROUP):
+                nc.tensor.transpose(
+                    turned[:, i * T : (i + 1) * T], result[:, i * P : (i + 1) * P], identity[:]
+                )
+            staged = work.tile([P, BANK], F32, name="staged")
+            nc.scalar.copy(staged[:], turned[:])
+            nc.sync.dma_start(
+                out.rearrange("(b p) t -> p b t", p=P)[:, g * GROUP : (g + 1) * GROUP, :],
+                staged[:].rearrange("p (b t) -> p b t", t=T),
+            )
 
         e_of = {0: weights(0)}
         for d in range(BLOCKS):
             if d + AHEAD < BLOCKS:
                 raw[d + AHEAD] = new_score_banks(d + AHEAD)
                 for c in range(BLOCKS):
-                    score_matmuls(raw[d + AHEAD], d + AHEAD, c)
+                    score_matmuls(d + AHEAD, c)
             if d + 1 < BLOCKS:
                 e_of[d + 1] = weights(d + 1)
+            if d % GROUP == 0 and d > 0:
+                finish(d // GROUP - 1)
             attend(d, e_of[d])
+        finish(BLOCKS // GROUP - 1)

@@ -157,7 +157,7 @@ def tile_graphattentionencoder_kernel(tc, x, wna, offs, out):
             top = work.tile([P, T], F32, name="top")
             nc.vector.tensor_reduce(top[:], per_target(z[:]), axis=AXIS.X, op=ALU.max)
             shifted = work.tile([P, N], F32, name="shifted")
-            nc.vector.tensor_tensor(
+            nc.gpsimd.tensor_tensor(
                 per_target(shifted[:]), per_target(z[:]), over_neighbours(top[:]), ALU.subtract
             )
             e = work.tile([P, N], F32, name="e")
@@ -183,21 +183,25 @@ def tile_graphattentionencoder_kernel(tc, x, wna, offs, out):
                 summed[g] = side_banks.tile([P, BANK], F32, name=f"summed{g}", tag="side")
             sum_over_neighbours(summed[g], d, weighted)
 
-        def finish(g):
+        def finish(first, end):
+            g = first // GROUP
+            width = (end - first) * P
+            cols = slice((first % GROUP) * P, (first % GROUP) * P + width)
             result = work.tile([P, BANK], F32, name="result")
             nc.vector.scalar_tensor_tensor(
-                result[:], summed[g][:], 1.0 - BETA, inverse[g][:], ALU.mult, ALU.mult
+                result[:, 0:width], summed[g][:, cols], 1.0 - BETA, inverse[g][:, cols],
+                ALU.mult, ALU.mult,
             )
-            turned = score_banks.tile([P, BANK], F32, name=f"turned{g}", tag="raw0")
-            for i in range(GROUP):
+            turned = score_banks.tile([P, BANK], F32, name=f"turned{first}", tag="raw0")
+            for i in range(end - first):
                 nc.tensor.transpose(
                     turned[:, i * T : (i + 1) * T], result[:, i * P : (i + 1) * P], identity[:]
                 )
             staged = work.tile([P, BANK], F32, name="staged")
-            nc.scalar.copy(staged[:], turned[:])
+            nc.scalar.copy(staged[:, 0:width], turned[:, 0:width])
             nc.sync.dma_start(
-                out.rearrange("(b p) t -> p b t", p=P)[:, g * GROUP : (g + 1) * GROUP, :],
-                staged[:].rearrange("p (b t) -> p b t", t=T),
+                out.rearrange("(b p) t -> p b t", p=P)[:, first:end, :],
+                staged[:, 0:width].rearrange("p (b t) -> p b t", t=T),
             )
 
         e_of = {0: weights(0)}
@@ -209,6 +213,7 @@ def tile_graphattentionencoder_kernel(tc, x, wna, offs, out):
             if d + 1 < BLOCKS:
                 e_of[d + 1] = weights(d + 1)
             if d % GROUP == 0 and d > 0:
-                finish(d // GROUP - 1)
+                finish(d - GROUP, d)
             attend(d, e_of[d])
-        finish(BLOCKS // GROUP - 1)
+        finish(BLOCKS - GROUP, BLOCKS - 1)
+        finish(BLOCKS - 1, BLOCKS)

@@ -157,7 +157,7 @@ def tile_graphattentionencoder_kernel(tc, x, wna, offs, out):
             top = work.tile([P, T], F32, name="top")
             nc.vector.tensor_reduce(top[:], per_target(z[:]), axis=AXIS.X, op=ALU.max)
             shifted = work.tile([P, N], F32, name="shifted")
-            nc.gpsimd.tensor_tensor(
+            nc.vector.tensor_tensor(
                 per_target(shifted[:]), per_target(z[:]), over_neighbours(top[:]), ALU.subtract
             )
             e = work.tile([P, N], F32, name="e")

@@ -19,7 +19,7 @@ BANK = 512
 HALVES = N // BANK
 AHEAD = 3
 GROUP = BANK // P
-LATE = 5
+PACED = 2
 
 BETA, ALPHA, MAX_DIST, EPS = 0.2, 0.3, 250.0, 1e-8
 
@@ -30,20 +30,24 @@ def tile_graphattentionencoder_kernel(tc, x, wna, offs, out):
     nc = tc.nc
     with (
         tc.tile_pool(name="held", bufs=1) as held,
-        tc.tile_pool(name="diffs", bufs=LATE + 2) as diffs,
+        tc.tile_pool(name="diffs", bufs=BLOCKS) as diffs,
         tc.tile_pool(name="work", bufs=2) as work,
         tc.psum_pool(name="side_banks", bufs=2) as side_banks,
         tc.psum_pool(name="score_banks", bufs=AHEAD) as score_banks,
     ):
         offsets = held.tile([P, N // 16], U16, name="offsets")
         nc.sync.dma_start(offsets[:], offs)
+        all_targets = x.rearrange("(c p) s -> p c s", p=P)[:, :, 0:T]
+        early_targets = held.tile([P, BLOCKS, T], F32, name="early_targets")
+        nc.sync.dma_start(early_targets[:], all_targets)
         x_blk = [held.tile([P, S], F32, name=f"x{c}") for c in range(BLOCKS)]
         w_blk = [held.tile([P, C], BF16, name=f"w{c}") for c in range(BLOCKS)]
         for c in range(BLOCKS):
-            queue = nc.sync if c % 2 == 0 else nc.scalar
-            queue.dma_start(x_blk[c][:], x[c * P : (c + 1) * P, :])
+            nc.sync.dma_start(x_blk[c][:], x[c * P : (c + 1) * P, :])
+        targets = held.tile([P, BLOCKS, T], F32, name="targets")
+        nc.sync.dma_start(targets[:], all_targets)
         for c in range(BLOCKS):
-            nc.gpsimd.dma_start(w_blk[c][:], wna[c * P : (c + 1) * P, :])
+            nc.sync.dma_start(w_blk[c][:], wna[c * P : (c + 1) * P, :])
 
         ones = held.tile([P, P], BF16, name="ones")
         nc.gpsimd.memset(ones[:], 1.0)
@@ -84,8 +88,8 @@ def tile_graphattentionencoder_kernel(tc, x, wna, offs, out):
         diff = {}
 
         def negate_target(c):
-            neg_target[c] = work.tile([P, N], F32, name=f"neg_target{c}", tag="neg_target", bufs=3)
-            nc.scalar.mul(per_target(neg_target[c][:]), over_neighbours(x_blk[c][:, 0:T]), -1.0)
+            neg_target[c] = diffs.tile([P, N], F32, name=f"neg_target{c}", tag="neg_target")
+            nc.scalar.mul(per_target(neg_target[c][:]), over_neighbours(early_targets[:, c, :]), -1.0)
 
         def look_up_diff(c):
             diff[c] = diffs.tile([P, N], F32, name=f"diff{c}", tag="diff")
@@ -105,25 +109,21 @@ def tile_graphattentionencoder_kernel(tc, x, wna, offs, out):
             nc.vector.tensor_tensor(
                 per_target(nbr[c][:]),
                 per_target(diff[c][:]),
-                over_neighbours(x_blk[c][:, 0:T]),
+                over_neighbours(targets[:, c, :]),
                 ALU.add,
             )
 
-        negate_target(0)
-        negate_target(1)
+        for c in range(BLOCKS):
+            negate_target(c)
         for c in range(BLOCKS):
             look_up_diff(c)
-            if c + 2 < BLOCKS:
-                negate_target(c + 2)
             sum_squares(c)
-            if c >= LATE:
-                pick(c - LATE)
-                for d in range(AHEAD):
-                    score_matmuls(d, c - LATE)
-        for c in range(BLOCKS - LATE, BLOCKS):
+        for c in range(BLOCKS):
             pick(c)
-        for d in range(AHEAD):
-            for c in range(BLOCKS - LATE, BLOCKS):
+            for d in range(PACED):
+                score_matmuls(d, c)
+        for d in range(PACED, AHEAD):
+            for c in range(BLOCKS):
                 score_matmuls(d, c)
 
         dist = held.tile([P, N], F32, name="dist")

@@ -19,6 +19,8 @@ BANK = 512
 HALVES = N // BANK
 AHEAD = 3
 GROUP = BANK // P
+LAST = BLOCKS - 1
+CLOSING = 3
 PACED = 2
 
 BETA, ALPHA, MAX_DIST, EPS = 0.2, 0.3, 250.0, 1e-8
@@ -120,7 +122,10 @@ def tile_graphattentionencoder_kernel(tc, x, wna, offs, out):
             sum_squares(c)
         for c in range(BLOCKS):
             pick(c)
-            for d in range(PACED):
+            for d in range(min(PACED, c + 1)):
+                score_matmuls(d, c - d)
+        for d in range(1, PACED):
+            for c in range(BLOCKS - d, BLOCKS):
                 score_matmuls(d, c)
         for d in range(PACED, AHEAD):
             for c in range(BLOCKS):
@@ -160,7 +165,7 @@ def tile_graphattentionencoder_kernel(tc, x, wna, offs, out):
             nc.vector.tensor_tensor(
                 per_target(shifted[:]), per_target(z[:]), over_neighbours(top[:]), ALU.subtract
             )
-            e = work.tile([P, N], F32, name="e")
+            e = work.tile([P, N], F32, name="e", bufs=CLOSING)
             nc.scalar.activation(e[:], shifted[:], ACT.Exp)
             g = d // GROUP
             if d % GROUP == 0:
@@ -173,11 +178,15 @@ def tile_graphattentionencoder_kernel(tc, x, wna, offs, out):
                 nc.scalar.activation(inverse[g][:], log_total[:], ACT.Exp, scale=-1.0)
             return e
 
-        def attend(d, e):
+        def look_up_weighted(d, e):
             weighted = work.tile([P, N], F32, name="weighted")
             nc.vector.tensor_tensor(
                 weighted[:], x_blk[d][:].indirect(offsets[:]), e[:], ALU.mult
             )
+            return weighted
+
+        def attend(d, e):
+            weighted = look_up_weighted(d, e)
             g = d // GROUP
             if d % GROUP == 0:
                 summed[g] = side_banks.tile([P, BANK], F32, name=f"summed{g}", tag="side")
@@ -204,16 +213,37 @@ def tile_graphattentionencoder_kernel(tc, x, wna, offs, out):
                 staged[:, 0:width].rearrange("p (b t) -> p b t", t=T),
             )
 
-        e_of = {0: weights(0)}
-        for d in range(BLOCKS):
+        e_of = {}
+
+        def prepare(d):
+            e_of[d] = weights(d)
             if d + AHEAD < BLOCKS:
                 raw[d + AHEAD] = new_score_banks(d + AHEAD)
                 for c in range(BLOCKS):
                     score_matmuls(d + AHEAD, c)
-            if d + 1 < BLOCKS:
-                e_of[d + 1] = weights(d + 1)
+
+        prepare(0)
+        for d in range(LAST):
+            if d < BLOCKS - CLOSING:
+                prepare(d + 1)
+            if d == BLOCKS - CLOSING:
+                for later in range(d + 1, BLOCKS):
+                    prepare(later)
             if d % GROUP == 0 and d > 0:
                 finish(d - GROUP, d)
             attend(d, e_of[d])
-        finish(BLOCKS - GROUP, BLOCKS - 1)
-        finish(BLOCKS - 1, BLOCKS)
+        finish(BLOCKS - GROUP, LAST)
+        inverse_turned = score_banks.tile([P, BANK], F32, name="inverse_turned", tag="raw1")
+        nc.tensor.transpose(
+            inverse_turned[:, 0:T],
+            inverse[LAST // GROUP][:, (LAST % GROUP) * P : (LAST % GROUP + 1) * P],
+            identity[:],
+        )
+        weighted = look_up_weighted(LAST, e_of[LAST])
+        summed_last = work.tile([P, T], F32, name="summed_last")
+        nc.vector.tensor_reduce(summed_last[:], per_target(weighted[:]), axis=AXIS.X, op=ALU.add)
+        result_last = work.tile([P, T], F32, name="result_last")
+        nc.vector.scalar_tensor_tensor(
+            result_last[:], summed_last[:], 1.0 - BETA, inverse_turned[:, 0:T], ALU.mult, ALU.mult
+        )
+        nc.sync.dma_start(out[LAST * P : (LAST + 1) * P, :], result_last[:])

@@ -162,7 +162,8 @@ def tile_graphattentionencoder_kernel(tc, x, wna, offs, out):
             top = work.tile([P, T], F32, name="top")
             nc.vector.tensor_reduce(top[:], per_target(z[:]), axis=AXIS.X, op=ALU.max)
             shifted = work.tile([P, N], F32, name="shifted")
-            nc.vector.tensor_tensor(
+            engine = nc.gpsimd if d == LAST - 1 else nc.vector
+            engine.tensor_tensor(
                 per_target(shifted[:]), per_target(z[:]), over_neighbours(top[:]), ALU.subtract
             )
             e = work.tile([P, N], F32, name="e", bufs=CLOSING)

@@ -20,7 +20,7 @@ HALVES = N // BANK
 AHEAD = 3
 GROUP = BANK // P
 LAST = BLOCKS - 1
-CLOSING = 3
+CLOSING = 4
 PACED = 2
 
 BETA, ALPHA, MAX_DIST, EPS = 0.2, 0.3, 250.0, 1e-8
@@ -162,7 +162,7 @@ def tile_graphattentionencoder_kernel(tc, x, wna, offs, out):
             top = work.tile([P, T], F32, name="top")
             nc.vector.tensor_reduce(top[:], per_target(z[:]), axis=AXIS.X, op=ALU.max)
             shifted = work.tile([P, N], F32, name="shifted")
-            engine = nc.gpsimd if d == LAST - 1 else nc.vector
+            engine = nc.gpsimd if BLOCKS - CLOSING < d < LAST else nc.vector
             engine.tensor_tensor(
                 per_target(shifted[:]), per_target(z[:]), over_neighbours(top[:]), ALU.subtract
             )
@@ -241,9 +241,9 @@ def tile_graphattentionencoder_kernel(tc, x, wna, offs, out):
             identity[:],
         )
         weighted = look_up_weighted(LAST, e_of[LAST])
-        summed_last = work.tile([P, T], F32, name="summed_last")
+        summed_last = work.tile([P, T], F32, name="summed_last", bufs=1)
         nc.vector.tensor_reduce(summed_last[:], per_target(weighted[:]), axis=AXIS.X, op=ALU.add)
-        result_last = work.tile([P, T], F32, name="result_last")
+        result_last = work.tile([P, T], F32, name="result_last", bufs=1)
         nc.vector.scalar_tensor_tensor(
             result_last[:], summed_last[:], 1.0 - BETA, inverse_turned[:, 0:T], ALU.mult, ALU.mult
         )

@@ -21,6 +21,7 @@ AHEAD = 3
 GROUP = BANK // P
 LAST = BLOCKS - 1
 CLOSING = 4
+EARLY = 2
 PACED = 2
 
 BETA, ALPHA, MAX_DIST, EPS = 0.2, 0.3, 250.0, 1e-8
@@ -41,20 +42,38 @@ def tile_graphattentionencoder_kernel(tc, x, wna, offs, out):
         nc.sync.dma_start(offsets[:], offs)
         all_targets = x.rearrange("(c p) s -> p c s", p=P)[:, :, 0:T]
         early_targets = held.tile([P, BLOCKS, T], F32, name="early_targets")
-        nc.sync.dma_start(early_targets[:], all_targets)
         x_blk = [held.tile([P, S], F32, name=f"x{c}") for c in range(BLOCKS)]
         w_blk = [held.tile([P, C], BF16, name=f"w{c}") for c in range(BLOCKS)]
-        for c in range(BLOCKS):
-            nc.sync.dma_start(x_blk[c][:], x[c * P : (c + 1) * P, :])
-        targets = held.tile([P, BLOCKS, T], F32, name="targets")
-        nc.sync.dma_start(targets[:], all_targets)
-        for c in range(BLOCKS):
+
+        def load_weights(c):
             nc.sync.dma_start(w_blk[c][:], wna[c * P : (c + 1) * P, :])
+
+        late_targets = held.tile([P, BLOCKS, T], F32, name="late_targets")
+
+        def load_late_targets(first, end):
+            nc.sync.dma_start(late_targets[:, first:end, :], all_targets[:, first:end, :])
+
+        nc.sync.dma_start(early_targets[:, 0:1, :], all_targets[:, 0:1, :])
+        for c in range(BLOCKS):
+            if c == LAST - EARLY:
+                load_weights(0)
+            nc.sync.dma_start(x_blk[c][:], x[c * P : (c + 1) * P, :])
+            if c == 0:
+                nc.sync.dma_start(early_targets[:, 1:BLOCKS, :], all_targets[:, 1:BLOCKS, :])
+            if LAST - EARLY <= c < LAST:
+                early = c - (LAST - EARLY)
+                load_late_targets(early, early + 1)
+                load_weights(early + 1)
+        load_late_targets(EARLY, BLOCKS)
+        for c in range(EARLY + 1, BLOCKS):
+            load_weights(c)
 
         ones = held.tile([P, P], BF16, name="ones")
         nc.gpsimd.memset(ones[:], 1.0)
         identity = held.tile([P, P], F32, name="identity")
         make_identity(nc, identity[:])
+        root_of_one = held.tile([P, 2], F32, name="root_of_one")
+        nc.scalar.activation(root_of_one[:], ones[:, 0:2], ACT.Sqrt)
 
         def per_target(tile_pn):
             return tile_pn.rearrange("p (t k) -> p t k", k=K)
@@ -111,7 +130,7 @@ def tile_graphattentionencoder_kernel(tc, x, wna, offs, out):
             nc.vector.tensor_tensor(
                 per_target(nbr[c][:]),
                 per_target(diff[c][:]),
-                over_neighbours(targets[:, c, :]),
+                over_neighbours(late_targets[:, c, :]),
                 ALU.add,
             )
 
@@ -120,15 +139,21 @@ def tile_graphattentionencoder_kernel(tc, x, wna, offs, out):
         for c in range(BLOCKS):
             look_up_diff(c)
             sum_squares(c)
-        for c in range(BLOCKS):
+            if LAST - EARLY <= c < LAST:
+                early = c - (LAST - EARLY)
+                pick(early)
+                for d in range(AHEAD):
+                    score_matmuls(d, early)
+        for c in range(EARLY, BLOCKS):
             pick(c)
-            for d in range(min(PACED, c + 1)):
-                score_matmuls(d, c - d)
+            for d in range(PACED):
+                if c - d >= EARLY:
+                    score_matmuls(d, c - d)
         for d in range(1, PACED):
             for c in range(BLOCKS - d, BLOCKS):
                 score_matmuls(d, c)
         for d in range(PACED, AHEAD):
-            for c in range(BLOCKS):
+            for c in range(EARLY, BLOCKS):
                 score_matmuls(d, c)
 
         dist = held.tile([P, N], F32, name="dist")

@@ -20,8 +20,10 @@ HALVES = N // BANK
 AHEAD = 3
 GROUP = BANK // P
 LAST = BLOCKS - 1
-CLOSING = 4
-EARLY = 2
+RUNS = [[0], [1, 2], [3, 4], [5, 6, 7]]
+ENDS = [run[-1] for run in RUNS]
+SOON = 4
+EARLY = 4
 PACED = 2
 
 BETA, ALPHA, MAX_DIST, EPS = 0.2, 0.3, 250.0, 1e-8
@@ -58,8 +60,9 @@ def tile_graphattentionencoder_kernel(tc, x, wna, offs, out):
             if c == LAST - EARLY:
                 load_weights(0)
             nc.sync.dma_start(x_blk[c][:], x[c * P : (c + 1) * P, :])
-            if c == 0:
-                nc.sync.dma_start(early_targets[:, 1:BLOCKS, :], all_targets[:, 1:BLOCKS, :])
+            if c < 2:
+                cols = slice(1, SOON) if c == 0 else slice(SOON, BLOCKS)
+                nc.sync.dma_start(early_targets[:, cols, :], all_targets[:, cols, :])
             if LAST - EARLY <= c < LAST:
                 early = c - (LAST - EARLY)
                 load_late_targets(early, early + 1)
@@ -109,11 +112,11 @@ def tile_graphattentionencoder_kernel(tc, x, wna, offs, out):
         diff = {}
 
         def negate_target(c):
-            neg_target[c] = diffs.tile([P, N], F32, name=f"neg_target{c}", tag="neg_target")
+            neg_target[c] = diffs.tile([P, N], F32, name=f"neg_target{c}", tag="neg_target", bufs=5)
             nc.scalar.mul(per_target(neg_target[c][:]), over_neighbours(early_targets[:, c, :]), -1.0)
 
         def look_up_diff(c):
-            diff[c] = diffs.tile([P, N], F32, name=f"diff{c}", tag="diff")
+            diff[c] = diffs.tile([P, N], F32, name=f"diff{c}", tag="diff", bufs=BLOCKS - EARLY + 1)
             nc.vector.tensor_tensor(
                 diff[c][:], x_blk[c][:].indirect(offsets[:]), neg_target[c][:], ALU.add
             )
@@ -167,7 +170,9 @@ def tile_graphattentionencoder_kernel(tc, x, wna, offs, out):
 
         total = {}
         summed = {}
-        inverse = {}
+        shifted = {}
+        e = {}
+        weighted = {}
 
         def sum_over_neighbours(bank, d, tile_pn):
             for k in range(K):
@@ -184,92 +189,78 @@ def tile_graphattentionencoder_kernel(tc, x, wna, offs, out):
             z = work.tile([P, N], F32, name="z")
             for h, cols in enumerate(halves()):
                 nc.vector.tensor_tensor(z[:, cols], raw[d][h][:], damp[:, cols], ALU.mult)
-            top = work.tile([P, T], F32, name="top")
-            nc.vector.tensor_reduce(top[:], per_target(z[:]), axis=AXIS.X, op=ALU.max)
-            shifted = work.tile([P, N], F32, name="shifted")
-            engine = nc.gpsimd if BLOCKS - CLOSING < d < LAST else nc.vector
-            engine.tensor_tensor(
-                per_target(shifted[:]), per_target(z[:]), over_neighbours(top[:]), ALU.subtract
-            )
-            e = work.tile([P, N], F32, name="e", bufs=CLOSING)
-            nc.scalar.activation(e[:], shifted[:], ACT.Exp)
-            g = d // GROUP
-            if d % GROUP == 0:
-                total[g] = side_banks.tile([P, BANK], F32, name=f"total{g}", tag="side")
-            sum_over_neighbours(total[g], d, e)
-            if d % GROUP == GROUP - 1:
-                log_total = work.tile([P, BANK], F32, name="log_total")
-                nc.scalar.activation(log_total[:], total[g][:], ACT.Ln)
-                inverse[g] = work.tile([P, BANK], F32, name=f"inverse{g}", tag="inverse")
-                nc.scalar.activation(inverse[g][:], log_total[:], ACT.Exp, scale=-1.0)
-            return e
-
-        def look_up_weighted(d, e):
-            weighted = work.tile([P, N], F32, name="weighted")
-            nc.vector.tensor_tensor(
-                weighted[:], x_blk[d][:].indirect(offsets[:]), e[:], ALU.mult
-            )
-            return weighted
-
-        def attend(d, e):
-            weighted = look_up_weighted(d, e)
-            g = d // GROUP
-            if d % GROUP == 0:
-                summed[g] = side_banks.tile([P, BANK], F32, name=f"summed{g}", tag="side")
-            sum_over_neighbours(summed[g], d, weighted)
-
-        def finish(first, end):
-            g = first // GROUP
-            width = (end - first) * P
-            cols = slice((first % GROUP) * P, (first % GROUP) * P + width)
-            result = work.tile([P, BANK], F32, name="result")
-            nc.vector.scalar_tensor_tensor(
-                result[:, 0:width], summed[g][:, cols], 1.0 - BETA, inverse[g][:, cols],
-                ALU.mult, ALU.mult,
-            )
-            turned = score_banks.tile([P, BANK], F32, name=f"turned{first}", tag="raw0")
-            for i in range(end - first):
-                nc.tensor.transpose(
-                    turned[:, i * T : (i + 1) * T], result[:, i * P : (i + 1) * P], identity[:]
-                )
-            staged = work.tile([P, BANK], F32, name="staged")
-            nc.scalar.copy(staged[:, 0:width], turned[:, 0:width])
-            nc.sync.dma_start(
-                out.rearrange("(b p) t -> p b t", p=P)[:, first:end, :],
-                staged[:, 0:width].rearrange("p (b t) -> p b t", t=T),
-            )
-
-        e_of = {}
-
-        def prepare(d):
-            e_of[d] = weights(d)
             if d + AHEAD < BLOCKS:
                 raw[d + AHEAD] = new_score_banks(d + AHEAD)
                 for c in range(BLOCKS):
                     score_matmuls(d + AHEAD, c)
+            top = work.tile([P, T], F32, name="top")
+            nc.vector.tensor_reduce(top[:], per_target(z[:]), axis=AXIS.X, op=ALU.max)
+            shifted[d] = work.tile([P, N], F32, name=f"shifted{d}", tag="shifted")
+            engine = nc.vector if d in ENDS else nc.gpsimd
+            engine.tensor_tensor(
+                per_target(shifted[d][:]), per_target(z[:]), over_neighbours(top[:]), ALU.subtract
+            )
+            e[d] = work.tile([P, N], F32, name=f"e{d}", tag="e", bufs=6)
+            nc.scalar.activation(e[d][:], shifted[d][:], ACT.Exp)
 
-        prepare(0)
-        for d in range(LAST):
-            if d < BLOCKS - CLOSING:
-                prepare(d + 1)
-            if d == BLOCKS - CLOSING:
-                for later in range(d + 1, BLOCKS):
-                    prepare(later)
-            if d % GROUP == 0 and d > 0:
-                finish(d - GROUP, d)
-            attend(d, e_of[d])
-        finish(BLOCKS - GROUP, LAST)
-        inverse_turned = score_banks.tile([P, BANK], F32, name="inverse_turned", tag="raw1")
-        nc.tensor.transpose(
-            inverse_turned[:, 0:T],
-            inverse[LAST // GROUP][:, (LAST % GROUP) * P : (LAST % GROUP + 1) * P],
-            identity[:],
+        def look_up_weighted(d):
+            weighted[d] = work.tile([P, N], F32, name=f"weighted{d}", tag="weighted", bufs=4)
+            nc.vector.tensor_tensor(
+                weighted[d][:], x_blk[d][:].indirect(offsets[:]), e[d][:], ALU.mult
+            )
+
+        def sum_weights(d):
+            if d % GROUP == 0:
+                total[d // GROUP] = new_sum_bank(d, "total", "raw0")
+            sum_over_neighbours(total[d // GROUP], d, e[d])
+
+        def sum_weighted(d):
+            if d % GROUP == 0:
+                summed[d // GROUP] = new_sum_bank(d, "summed", "raw1")
+            sum_over_neighbours(summed[d // GROUP], d, weighted[d])
+
+        def new_sum_bank(d, name, score_tag):
+            if d < GROUP:
+                return side_banks.tile([P, BANK], F32, name=f"{name}{d}", tag="side")
+            return score_banks.tile([P, BANK], F32, name=f"{name}{d}", tag=score_tag)
+
+        def finish(g):
+            result = work.tile([P, BANK], F32, name="result")
+            nc.vector.scalar_tensor_tensor(
+                result[:], summed[g][:], 1.0 - BETA, inverse[:, g, :], ALU.mult, ALU.mult
+            )
+            turned = score_banks.tile([P, BANK], F32, name=f"turned{g}", tag="raw0")
+            for i in range(GROUP):
+                nc.tensor.transpose(
+                    turned[:, i * T : (i + 1) * T], result[:, i * P : (i + 1) * P], identity[:]
+                )
+            staged = work.tile([P, BANK], F32, name="staged")
+            nc.scalar.copy(staged[:], turned[:])
+            nc.sync.dma_start(
+                out.rearrange("(b p) t -> p b t", p=P)[:, g * GROUP : (g + 1) * GROUP, :],
+                staged[:].rearrange("p (b t) -> p b t", t=T),
+            )
+
+        for before, run in zip([[]] + RUNS, RUNS):
+            for d in run:
+                weights(d)
+            for d in before:
+                look_up_weighted(d)
+            for d in before:
+                sum_weights(d)
+                sum_weighted(d)
+        for d in RUNS[-1]:
+            sum_weights(d)
+        groups = BLOCKS // GROUP
+        log_total = shifted[LAST]
+        for g in range(groups):
+            nc.scalar.activation(log_total[:, g * BANK : (g + 1) * BANK], total[g][:], ACT.Ln)
+        inverse = work.tile([P, groups, BANK], F32, name="inverse", bufs=1)
+        nc.scalar.activation(
+            inverse[:].rearrange("p g d -> p (g d)"), log_total[:], ACT.Exp, scale=-1.0
         )
-        weighted = look_up_weighted(LAST, e_of[LAST])
-        summed_last = work.tile([P, T], F32, name="summed_last", bufs=1)
-        nc.vector.tensor_reduce(summed_last[:], per_target(weighted[:]), axis=AXIS.X, op=ALU.add)
-        result_last = work.tile([P, T], F32, name="result_last", bufs=1)
-        nc.vector.scalar_tensor_tensor(
-            result_last[:], summed_last[:], 1.0 - BETA, inverse_turned[:, 0:T], ALU.mult, ALU.mult
-        )
-        nc.sync.dma_start(out[LAST * P : (LAST + 1) * P, :], result_last[:])
+        for d in RUNS[-1]:
+            look_up_weighted(d)
+            sum_weighted(d)
+        for g in range(groups):
+            finish(g)

@@ -21,9 +21,8 @@ AHEAD = 3
 GROUP = BANK // P
 LAST = BLOCKS - 1
 RUNS = [[0], [1, 2], [3, 4], [5, 6, 7]]
-ENDS = [run[-1] for run in RUNS]
 SOON = 4
-EARLY = 4
+EARLY = 3
 PACED = 2
 
 BETA, ALPHA, MAX_DIST, EPS = 0.2, 0.3, 250.0, 1e-8
@@ -82,7 +81,7 @@ def tile_graphattentionencoder_kernel(tc, x, wna, offs, out):
             return tile_pn.rearrange("p (t k) -> p t k", k=K)
 
         def over_neighbours(tile_pt):
-            return tile_pt.unsqueeze(2).to_broadcast([P, T, K])
+            return tile_pt.unsqueeze(2).to_broadcast([P, tile_pt.shape[1], K])
 
         def halves():
             return [slice(h * BANK, (h + 1) * BANK) for h in range(HALVES)]
@@ -123,19 +122,22 @@ def tile_graphattentionencoder_kernel(tc, x, wna, offs, out):
 
         def sum_squares(c):
             square = work.tile([P, N], BF16, name="square")
-            nc.scalar.activation(square[:], diff[c][:], ACT.Square)
             for h, cols in enumerate(halves()):
+                nc.scalar.activation(square[:, cols], diff[c][:, cols], ACT.Square)
                 nc.tensor.matmul(
                     dist2[h][:], ones[:], square[:, cols], start=(c == 0), stop=(c == BLOCKS - 1)
                 )
 
         def pick(c):
-            nc.vector.tensor_tensor(
-                per_target(nbr[c][:]),
-                per_target(diff[c][:]),
-                over_neighbours(late_targets[:, c, :]),
-                ALU.add,
-            )
+            parts = HALVES if c == LAST else 1
+            for part in range(parts):
+                targets = slice(part * T // parts, (part + 1) * T // parts)
+                nc.vector.tensor_tensor(
+                    per_target(nbr[c][:])[:, targets, :],
+                    per_target(diff[c][:])[:, targets, :],
+                    over_neighbours(late_targets[:, c, targets]),
+                    ALU.add,
+                )
 
         for c in range(BLOCKS):
             negate_target(c)
@@ -196,7 +198,7 @@ def tile_graphattentionencoder_kernel(tc, x, wna, offs, out):
             top = work.tile([P, T], F32, name="top")
             nc.vector.tensor_reduce(top[:], per_target(z[:]), axis=AXIS.X, op=ALU.max)
             shifted[d] = work.tile([P, N], F32, name=f"shifted{d}", tag="shifted")
-            engine = nc.vector if d in ENDS else nc.gpsimd
+            engine = nc.gpsimd if d in RUNS[-1][:-1] else nc.vector
             engine.tensor_tensor(
                 per_target(shifted[d][:]), per_target(z[:]), over_neighbours(top[:]), ALU.subtract
             )

@@ -23,7 +23,6 @@ LAST = BLOCKS - 1
 RUNS = [[0], [1, 2], [3, 4], [5, 6, 7]]
 SOON = 4
 EARLY = 3
-PACED = 2
 
 BETA, ALPHA, MAX_DIST, EPS = 0.2, 0.3, 250.0, 1e-8
 
@@ -151,13 +150,8 @@ def tile_graphattentionencoder_kernel(tc, x, wna, offs, out):
                     score_matmuls(d, early)
         for c in range(EARLY, BLOCKS):
             pick(c)
-            for d in range(PACED):
-                if c - d >= EARLY:
-                    score_matmuls(d, c - d)
-        for d in range(1, PACED):
-            for c in range(BLOCKS - d, BLOCKS):
-                score_matmuls(d, c)
-        for d in range(PACED, AHEAD):
+            score_matmuls(0, c)
+        for d in range(1, AHEAD):
             for c in range(EARLY, BLOCKS):
                 score_matmuls(d, c)
 
@@ -226,21 +220,25 @@ def tile_graphattentionencoder_kernel(tc, x, wna, offs, out):
                 return side_banks.tile([P, BANK], F32, name=f"{name}{d}", tag="side")
             return score_banks.tile([P, BANK], F32, name=f"{name}{d}", tag=score_tag)
 
-        def finish(g):
-            result = work.tile([P, BANK], F32, name="result")
+        def finish(first, end):
+            g = first // GROUP
+            width = (end - first) * P
+            cols = slice((first % GROUP) * P, (first % GROUP) * P + width)
+            result = work.tile([P, BANK], F32, name="result", bufs=3)
             nc.vector.scalar_tensor_tensor(
-                result[:], summed[g][:], 1.0 - BETA, inverse[:, g, :], ALU.mult, ALU.mult
+                result[:, 0:width], summed[g][:, cols], 1.0 - BETA, inverse[:, g, cols],
+                ALU.mult, ALU.mult,
             )
-            turned = score_banks.tile([P, BANK], F32, name=f"turned{g}", tag="raw0")
-            for i in range(GROUP):
+            turned = score_banks.tile([P, BANK], F32, name=f"turned{first}", tag="raw0")
+            for i in range(end - first):
                 nc.tensor.transpose(
                     turned[:, i * T : (i + 1) * T], result[:, i * P : (i + 1) * P], identity[:]
                 )
-            staged = work.tile([P, BANK], F32, name="staged")
-            nc.scalar.copy(staged[:], turned[:])
+            staged = work.tile([P, BANK], F32, name="staged", bufs=3)
+            nc.scalar.copy(staged[:, 0:width], turned[:, 0:width])
             nc.sync.dma_start(
-                out.rearrange("(b p) t -> p b t", p=P)[:, g * GROUP : (g + 1) * GROUP, :],
-                staged[:].rearrange("p (b t) -> p b t", t=T),
+                out.rearrange("(b p) t -> p b t", p=P)[:, first:end, :],
+                staged[:, 0:width].rearrange("p (b t) -> p b t", t=T),
             )
 
         for before, run in zip([[]] + RUNS, RUNS):
@@ -264,5 +262,6 @@ def tile_graphattentionencoder_kernel(tc, x, wna, offs, out):
         for d in RUNS[-1]:
             look_up_weighted(d)
             sum_weighted(d)
-        for g in range(groups):
-            finish(g)
+        finish(0, GROUP)
+        finish(GROUP, LAST)
+        finish(LAST, BLOCKS)

@@ -192,7 +192,7 @@ def tile_graphattentionencoder_kernel(tc, x, wna, offs, out):
             top = work.tile([P, T], F32, name="top")
             nc.vector.tensor_reduce(top[:], per_target(z[:]), axis=AXIS.X, op=ALU.max)
             shifted[d] = work.tile([P, N], F32, name=f"shifted{d}", tag="shifted")
-            engine = nc.gpsimd if d in RUNS[-1][:-1] else nc.vector
+            engine = nc.gpsimd if d in RUNS[0] + RUNS[-1][:-1] else nc.vector
             engine.tensor_tensor(
                 per_target(shifted[d][:]), per_target(z[:]), over_neighbours(top[:]), ALU.subtract
             )

import concourse.mybir as mybir
from concourse.masks import make_identity

F32 = mybir.dt.float32
BF16 = mybir.dt.bfloat16
U16 = mybir.dt.uint16
ALU = mybir.AluOpType
ACT = mybir.ActivationFunctionType
AXIS = mybir.AxisListType

P = 128
C = 1024
S = 2048
T = 128
K = 8
N = T * K
BLOCKS = C // P
BANK = 512
HALVES = N // BANK
AHEAD = 3
GROUP = BANK // P
LAST = BLOCKS - 1
RUNS = [[0], [1, 2], [3, 4], [5, 6, 7]]
SOON = 4
EARLY = 3

BETA, ALPHA, MAX_DIST, EPS = 0.2, 0.3, 250.0, 1e-8

FLOPS = 2 * C * C * N


def tile_graphattentionencoder_kernel(tc, x, wna, offs, out):
    nc = tc.nc
    with (
        tc.tile_pool(name="held", bufs=1) as held,
        tc.tile_pool(name="diffs", bufs=BLOCKS) as diffs,
        tc.tile_pool(name="work", bufs=2) as work,
        tc.psum_pool(name="side_banks", bufs=2) as side_banks,
        tc.psum_pool(name="score_banks", bufs=AHEAD) as score_banks,
    ):
        offsets = held.tile([P, N // 16], U16, name="offsets")
        nc.sync.dma_start(offsets[:], offs)
        all_targets = x.rearrange("(c p) s -> p c s", p=P)[:, :, 0:T]
        early_targets = held.tile([P, BLOCKS, T], F32, name="early_targets")
        x_blk = [held.tile([P, S], F32, name=f"x{c}") for c in range(BLOCKS)]
        w_blk = [held.tile([P, C], BF16, name=f"w{c}") for c in range(BLOCKS)]

        def load_weights(c):
            nc.sync.dma_start(w_blk[c][:], wna[c * P : (c + 1) * P, :])

        late_targets = held.tile([P, BLOCKS, T], F32, name="late_targets")

        def load_late_targets(first, end):
            nc.sync.dma_start(late_targets[:, first:end, :], all_targets[:, first:end, :])

        nc.sync.dma_start(early_targets[:, 0:1, :], all_targets[:, 0:1, :])
        for c in range(BLOCKS):
            if c == LAST - EARLY:
                load_weights(0)
            nc.sync.dma_start(x_blk[c][:], x[c * P : (c + 1) * P, :])
            if c < 2:
                cols = slice(1, SOON) if c == 0 else slice(SOON, BLOCKS)
                nc.sync.dma_start(early_targets[:, cols, :], all_targets[:, cols, :])
            if LAST - EARLY <= c < LAST:
                early = c - (LAST - EARLY)
                load_late_targets(early, early + 1)
                load_weights(early + 1)
        load_late_targets(EARLY, BLOCKS)
        for c in range(EARLY + 1, BLOCKS):
            load_weights(c)

        ones = held.tile([P, P], BF16, name="ones")
        nc.gpsimd.memset(ones[:], 1.0)
        identity = held.tile([P, P], F32, name="identity")
        make_identity(nc, identity[:])
        root_of_one = held.tile([P, 2], F32, name="root_of_one")
        nc.scalar.activation(root_of_one[:], ones[:, 0:2], ACT.Sqrt)

        def per_target(tile_pn):
            return tile_pn.rearrange("p (t k) -> p t k", k=K)

        def over_neighbours(tile_pt):
            return tile_pt.unsqueeze(2).to_broadcast([P, tile_pt.shape[1], K])

        def halves():
            return [slice(h * BANK, (h + 1) * BANK) for h in range(HALVES)]

        def new_score_banks(d):
            return [
                score_banks.tile([P, BANK], F32, name=f"raw{d}_{h}", tag=f"raw{h}")
                for h in range(HALVES)
            ]

        def score_matmuls(d, c):
            for h, cols in enumerate(halves()):
                nc.tensor.matmul(
                    raw[d][h][:],
                    w_blk[c][:, d * P : (d + 1) * P],
                    nbr[c][:, cols],
                    start=(c == 0),
                    stop=(c == BLOCKS - 1),
                )

        dist2 = [
            side_banks.tile([P, BANK], F32, name=f"dist2_{h}", tag="side") for h in range(HALVES)
        ]
        nbr = [held.tile([P, N], BF16, name=f"nbr{c}") for c in range(BLOCKS)]
        raw = {d: new_score_banks(d) for d in range(AHEAD)}
        neg_target = {}
        diff = {}

        def negate_target(c):
            neg_target[c] = diffs.tile([P, N], F32, name=f"neg_target{c}", tag="neg_target", bufs=5)
            nc.scalar.mul(per_target(neg_target[c][:]), over_neighbours(early_targets[:, c, :]), -1.0)

        def look_up_diff(c):
            diff[c] = diffs.tile([P, N], F32, name=f"diff{c}", tag="diff", bufs=BLOCKS - EARLY + 1)
            nc.vector.tensor_tensor(
                diff[c][:], x_blk[c][:].indirect(offsets[:]), neg_target[c][:], ALU.add
            )

        def sum_squares(c):
            square = work.tile([P, N], BF16, name="square")
            for h, cols in enumerate(halves()):
                nc.scalar.activation(square[:, cols], diff[c][:, cols], ACT.Square)
                nc.tensor.matmul(
                    dist2[h][:], ones[:], square[:, cols], start=(c == 0), stop=(c == BLOCKS - 1)
                )

        def pick(c):
            parts = HALVES if c == LAST else 1
            for part in range(parts):
                targets = slice(part * T // parts, (part + 1) * T // parts)
                nc.vector.tensor_tensor(
                    per_target(nbr[c][:])[:, targets, :],
                    per_target(diff[c][:])[:, targets, :],
                    over_neighbours(late_targets[:, c, targets]),
                    ALU.add,
                )

        for c in range(BLOCKS):
            negate_target(c)
        for c in range(BLOCKS):
            look_up_diff(c)
            sum_squares(c)
            if LAST - EARLY <= c < LAST:
                early = c - (LAST - EARLY)
                pick(early)
                for d in range(AHEAD):
                    score_matmuls(d, early)
        for c in range(EARLY, BLOCKS):
            pick(c)
            score_matmuls(0, c)
        for d in range(1, AHEAD):
            for c in range(EARLY, BLOCKS):
                score_matmuls(d, c)

        dist = held.tile([P, N], F32, name="dist")
        damp = held.tile([P, N], F32, name="damp")
        for h, cols in enumerate(halves()):
            nc.scalar.activation(dist[:, cols], dist2[h][:], ACT.Sqrt)
        for cols in halves():
            nc.scalar.activation(
                damp[:, cols], dist[:, cols], ACT.Exp, scale=-ALPHA / (MAX_DIST + EPS)
            )

        total = {}
        summed = {}
        shifted = {}
        e = {}
        weighted = {}

        def sum_over_neighbours(bank, d, tile_pn):
            for k in range(K):
                nc.tensor.matmul(
                    bank[:, (d % GROUP) * P : (d % GROUP + 1) * P],
                    per_target(tile_pn[:])[:, :, k],
                    identity[:],
                    is_transpose=True,
                    start=(k == 0),
                    stop=(k == K - 1),
                )

        def weights(d):
            z = work.tile([P, N], F32, name="z")
            for h, cols in enumerate(halves()):
                nc.vector.tensor_tensor(z[:, cols], raw[d][h][:], damp[:, cols], ALU.mult)
            if d + AHEAD < BLOCKS:
                raw[d + AHEAD] = new_score_banks(d + AHEAD)
                for c in range(BLOCKS):
                    score_matmuls(d + AHEAD, c)
            top = work.tile([P, T], F32, name="top")
            nc.vector.tensor_reduce(top[:], per_target(z[:]), axis=AXIS.X, op=ALU.max)
            shifted[d] = work.tile([P, N], F32, name=f"shifted{d}", tag="shifted")
            engine = nc.gpsimd if d in RUNS[0] + RUNS[-1][:-1] else nc.vector
            engine.tensor_tensor(
                per_target(shifted[d][:]), per_target(z[:]), over_neighbours(top[:]), ALU.subtract
            )
            e[d] = work.tile([P, N], F32, name=f"e{d}", tag="e", bufs=6)
            nc.scalar.activation(e[d][:], shifted[d][:], ACT.Exp)

        def look_up_weighted(d):
            weighted[d] = work.tile([P, N], F32, name=f"weighted{d}", tag="weighted", bufs=4)
            nc.vector.tensor_tensor(
                weighted[d][:], x_blk[d][:].indirect(offsets[:]), e[d][:], ALU.mult
            )

        def sum_weights(d):
            if d % GROUP == 0:
                total[d // GROUP] = new_sum_bank(d, "total", "raw0")
            sum_over_neighbours(total[d // GROUP], d, e[d])

        def sum_weighted(d):
            if d % GROUP == 0:
                summed[d // GROUP] = new_sum_bank(d, "summed", "raw1")
            sum_over_neighbours(summed[d // GROUP], d, weighted[d])

        def new_sum_bank(d, name, score_tag):
            if d < GROUP:
                return side_banks.tile([P, BANK], F32, name=f"{name}{d}", tag="side")
            return score_banks.tile([P, BANK], F32, name=f"{name}{d}", tag=score_tag)

        def finish(first, end):
            g = first // GROUP
            width = (end - first) * P
            cols = slice((first % GROUP) * P, (first % GROUP) * P + width)
            result = work.tile([P, BANK], F32, name="result", bufs=3)
            nc.vector.scalar_tensor_tensor(
                result[:, 0:width], summed[g][:, cols], 1.0 - BETA, inverse[:, g, cols],
                ALU.mult, ALU.mult,
            )
            turned = score_banks.tile([P, BANK], F32, name=f"turned{first}", tag="raw0")
            for i in range(end - first):
                nc.tensor.transpose(
                    turned[:, i * T : (i + 1) * T], result[:, i * P : (i + 1) * P], identity[:]
                )
            staged = work.tile([P, BANK], F32, name="staged", bufs=3)
            nc.scalar.copy(staged[:, 0:width], turned[:, 0:width])
            nc.sync.dma_start(
                out.rearrange("(b p) t -> p b t", p=P)[:, first:end, :],
                staged[:, 0:width].rearrange("p (b t) -> p b t", t=T),
            )

        for before, run in zip([[]] + RUNS, RUNS):
            for d in run:
                weights(d)
            for d in before:
                look_up_weighted(d)
            for d in before:
                sum_weights(d)
                sum_weighted(d)
        for d in RUNS[-1]:
            sum_weights(d)
        groups = BLOCKS // GROUP
        log_total = shifted[LAST]
        for g in range(groups):
            nc.scalar.activation(log_total[:, g * BANK : (g + 1) * BANK], total[g][:], ACT.Ln)
        inverse = work.tile([P, groups, BANK], F32, name="inverse", bufs=1)
        nc.scalar.activation(
            inverse[:].rearrange("p g d -> p (g d)"), log_total[:], ACT.Exp, scale=-1.0
        )
        for d in RUNS[-1]:
            look_up_weighted(d)
            sum_weighted(d)
        finish(0, GROUP)
        finish(GROUP, LAST)
        finish(LAST, BLOCKS)
